import numpy as np
import ml_dtypes


def mxq(x, axis, fmt="e4m3"):
    dtype, down = {"e4m3": (ml_dtypes.float8_e4m3fn, 7), "e5m2": (ml_dtypes.float8_e5m2, 14)}[fmt]
    v = np.moveaxis(np.asarray(x, np.float32).astype(ml_dtypes.bfloat16).astype(np.float64), axis, -1)
    blocks = v.reshape(v.shape[:-1] + (-1, 32))
    amax = np.abs(blocks).max(-1, keepdims=True)
    byte = np.maximum(np.where(amax > 0, np.frexp(amax)[1] - 1 + 127, 0) - down, 1)
    scale = np.exp2(byte - 127.0)
    codes = (blocks / scale).astype(np.float32).astype(dtype).astype(np.float64)
    return np.moveaxis((codes * scale).reshape(v.shape), -1, axis)


WIDE = False


def mx_kscale(k):
    if not WIDE:
        return np.ones(k)
    levels = np.array([10, -10, 5, -5, 0])
    a = np.random.permutation(np.resize(levels, k // 512 * 4)).reshape(k // 512, 4)
    idx = np.arange(k)
    return np.exp2(a[idx // 512, idx % 128 // 32])


BF16 = ml_dtypes.bfloat16


def bf(x):
    return np.asarray(x, np.float32).astype(BF16)


def f64(x):
    return np.asarray(x).astype(np.float64)


E2M1 = np.array([0.0, 0.5, 1.0, 1.5, 2.0, 3.0, 4.0, 6.0, -0.0, -0.5, -1.0, -1.5, -2.0, -3.0, -4.0, -6.0])


def pack_weight(w, fmt):
    k, n = w.shape
    w = f64(bf(w)).reshape(k // 32, 32, n)
    amax = np.abs(w).max(1)
    if fmt == "e4m3":
        byte = np.frexp(amax)[1] - 1 + 127 - 7
    else:
        mant, ex = np.frexp(amax / 6.0)
        byte = np.where(mant > 0.5, ex, ex - 1) + 127
    byte = np.clip(np.where(amax > 0, byte, 1), 1, 254)
    scaled = (w * np.exp2(127.0 - byte)[:, None, :]).reshape(k, n).astype(np.float32)
    by_word = np.ascontiguousarray(scaled.reshape(k // 512, 128, 4, n).transpose(0, 1, 3, 2))
    if fmt == "e4m3":
        words = by_word.astype(ml_dtypes.float8_e4m3fn).view(np.uint8)
    else:
        c = by_word.astype(ml_dtypes.float4_e2m1fn).view(np.uint8) & 0xF
        words = c[..., 0::2] | (c[..., 1::2] << 4)
    return np.ascontiguousarray(words), np.ascontiguousarray(byte.astype(np.uint8).reshape(k // 512, 16, n))


def unpack_weight(words, scales, fmt):
    g, p, n, _ = words.shape
    if fmt == "e4m3":
        vals = np.ascontiguousarray(words).view(ml_dtypes.float8_e4m3fn).astype(np.float64)
    else:
        nib = np.empty((g, p, n, 4), np.uint8)
        nib[..., 0::2] = words & 0xF
        nib[..., 1::2] = words >> 4
        vals = E2M1[nib]
    vals = vals * np.repeat(np.exp2(scales.astype(np.float64) - 127.0), 8, axis=1)[..., None]
    return vals.transpose(0, 1, 3, 2).reshape(g * 512, n)


B, T, D, N, R = 2, 512, 512, 4096, 32

MAX_ATTENTION_SCALE = 1.0
MIN_ATTENTION_SCALE = 0.05
SCALE_GROWTH_RATE = 0.02
G = 4.0
C0 = 12.0


def cloud(rows, u):
    z = np.random.standard_normal((rows, R))
    return (z @ u / np.sqrt(R) + np.random.standard_normal((rows, D))) * (G / np.sqrt(2.0 * D))


def setup_inputs():
    t = mx_kscale(N)
    u = np.random.standard_normal((R, D))
    x = cloud(B * T, u).reshape(B, T, D)
    positions = cloud(N, u)
    c = C0 * (1.0 + 0.03 * np.random.standard_normal(N)) - np.log(t)
    sign = np.where(np.random.standard_normal(N) < 0.0, -1.0, 1.0)
    temperature = sign * (np.sqrt(2.0) * G / c / MIN_ATTENTION_SCALE - 0.1)
    values = np.random.standard_normal((N, D)) * 0.15 * np.sqrt(N) * (t.mean() / t)[:, None]
    values_words, values_scales = pack_weight(values, "e4m3")
    return {"x": bf(x), "positions": bf(positions), "values_words": values_words, "values_scales": values_scales, "temperature": bf(temperature)}


def reference(x, positions, values_words, values_scales, temperature):
    x, positions, temperature = f64(x), f64(positions), f64(temperature)
    Bb, Tt, Dd = x.shape
    ages = np.zeros((positions.shape[0],))
    attention_scale = MIN_ATTENTION_SCALE + (MAX_ATTENTION_SCALE - MIN_ATTENTION_SCALE) * (1.0 - np.exp(-SCALE_GROWTH_RATE * ages))
    x_flat = x.reshape(-1, Dd)
    x2 = np.sum(x_flat * x_flat, axis=-1, keepdims=True)
    p2 = np.sum(positions * positions, axis=-1)[None, :]
    sq = x2 + p2 - 2.0 * (mxq(x_flat, 1, "e4m3") @ mxq(positions, 1, "e4m3").T)
    dists = np.sqrt(np.maximum(sq, 0.0))
    effective_temp = (np.abs(temperature) + 0.1) * attention_scale
    weights = np.exp(-dists / effective_temp[None, :])
    weights = weights / (np.sum(weights, axis=-1, keepdims=True) + 1e-8)
    out = mxq(weights, 1, "e4m3") @ unpack_weight(values_words, values_scales, "e4m3")
    return out.reshape(Bb, Tt, Dd)

@@ -1,0 +1,295 @@
+from contextlib import ExitStack
+
+import concourse.mybir as mybir
+from concourse.masks import make_identity
+
+F32 = mybir.dt.float32
+BF16 = mybir.dt.bfloat16
+I32 = mybir.dt.int32
+U32 = mybir.dt.uint32
+U8 = mybir.dt.uint8
+FP8X4 = mybir.dt.float8_e4m3fn_x4
+ALU = mybir.AluOpType
+ACT = mybir.ActivationFunctionType
+
+P = 128
+PACK = 4
+K_PASS = P * PACK
+ROWS = 1024
+FEATURES = 512
+ANCHORS = 4096
+ROW_TILES = ROWS // P
+GROUPS = ANCHORS // K_PASS
+BANK = 512
+ROW_HALVES = ROWS // BANK
+
+FLOPS = 2 * 2 * ROWS * ANCHORS * FEATURES
+
+
+def pack_two_tiles(nc, banks, ident, tile_a, tile_b, grouped):
+    bank = banks.tile([P, 2, 2, P], F32, tag="pack")
+    for a, tile in enumerate((tile_a, tile_b)):
+        words = tile.bitcast(F32)
+        for u in range(2):
+            nc.tensor.transpose(bank[:, a, u, :], words[:, u : FEATURES // 2 : 2], ident)
+    nc.scalar.copy(
+        out=grouped.bitcast(F32).rearrange("p (a c) u -> p a c u", a=2),
+        in_=bank[:].rearrange("p a u c -> p a c u"),
+    )
+
+
+def tile_multiscalegeometricattention_kernel(
+    tc, x, positions, values_words, values_scales, temperature, out
+):
+    nc = tc.nc
+    x_rows = x.flatten_outer_dims()
+    out_rows = out.flatten_outer_dims()
+
+    with ExitStack() as whole:
+        keep = whole.enter_context(tc.tile_pool(name="keep", bufs=1))
+
+        ident = keep.tile([P, P], F32)
+        make_identity(nc, ident[:])
+
+        z = [keep.tile([P, ANCHORS], F32, name="z%d" % rt) for rt in range(ROW_TILES)]
+        row_sum = keep.tile([P, ROW_TILES], F32)
+
+        v_words = keep.tile([P, GROUPS, FEATURES], U32, align_bytes=64)
+        v_scales = keep.tile([P, GROUPS, FEATURES], U8, align_bytes=64)
+        nc.vector.memset(v_scales[:].bitcast(I32), 0)
+
+        with ExitStack() as first:
+            once = first.enter_context(tc.tile_pool(name="once", bufs=1))
+            loads = first.enter_context(tc.tile_pool(name="loads", bufs=3))
+            stage = first.enter_context(tc.tile_pool(name="stage", bufs=2))
+            y_pool = first.enter_context(tc.tile_pool(name="y_pool", bufs=6))
+            pack_banks = first.enter_context(tc.psum_pool(name="pack_banks", bufs=2))
+            dot_banks = first.enter_context(tc.psum_pool(name="dot_banks", bufs=3))
+            turn_banks = first.enter_context(tc.psum_pool(name="turn_banks", bufs=3))
+
+            def load_positions(g):
+                pos = loads.tile([P, PACK, FEATURES], BF16, tag="pos")
+                nc.sync.dma_start(
+                    out=pos[:],
+                    in_=positions[g * K_PASS : (g + 1) * K_PASS, :].rearrange(
+                        "(p t) d -> p t d", t=PACK
+                    ),
+                )
+                return pos
+
+            x_sb = once.tile([P, ROW_TILES, FEATURES], BF16)
+            nc.sync.dma_start(out=x_sb[:], in_=x_rows.rearrange("(rt p) d -> p rt d", p=P))
+            temp = once.tile([P, GROUPS, PACK], BF16)
+            nc.sync.dma_start(
+                out=temp[:], in_=temperature.rearrange("(g p t) -> p g t", p=P, t=PACK)
+            )
+            pos_tiles = [load_positions(g) for g in range(3)]
+
+            temp_flat = temp[:].rearrange("p g t -> p (g t)")
+            tau = once.tile([P, GROUPS * PACK], F32)
+            nc.vector.scalar_tensor_tensor(
+                out=tau[:], in0=temp_flat, scalar=-1.0, in1=temp_flat, op0=ALU.mult, op1=ALU.max
+            )
+            nc.vector.tensor_scalar(
+                out=tau[:], in0=tau[:], scalar1=0.1, scalar2=0.05, op0=ALU.add, op1=ALU.mult
+            )
+            half_tau_sq = once.tile([P, GROUPS * PACK], F32)
+            nc.vector.scalar_tensor_tensor(
+                out=half_tau_sq[:], in0=tau[:], scalar=0.5, in1=tau[:], op0=ALU.mult, op1=ALU.mult
+            )
+            two_over_tau_sq = once.tile([P, GROUPS * PACK], F32)
+            nc.vector.reciprocal(out=two_over_tau_sq[:], in_=half_tau_sq[:])
+
+            x_sq = once.tile([P, ROW_TILES], F32)
+            for rt in range(ROW_TILES):
+                squares = stage.tile([P, FEATURES], BF16, tag="squares")
+                nc.scalar.activation(
+                    out=squares[:], in_=x_sb[:, rt, :], func=ACT.Square,
+                    accum_out=x_sq[:, rt : rt + 1],
+                )
+            half_x_sq = once.tile([P, ROW_TILES], F32)
+            nc.vector.tensor_scalar_mul(out=half_x_sq[:], in0=x_sq[:], scalar1=0.5)
+            half_x_sq_all = once.tile([P, ROWS], F32)
+            for half in range(ROW_HALVES):
+                spread = pack_banks.tile([P, BANK], F32, tag="pack")
+                for i in range(BANK // P):
+                    rt = half * (BANK // P) + i
+                    nc.tensor.transpose(
+                        spread[:, i * P : (i + 1) * P],
+                        half_x_sq[:, rt : rt + 1].to_broadcast([P, P]),
+                        ident[:],
+                    )
+                nc.scalar.copy(out=half_x_sq_all[:, half * BANK : (half + 1) * BANK], in_=spread[:])
+
+            x_grouped = once.tile([P, ROWS, PACK], BF16, align_bytes=64)
+            for rt in range(0, ROW_TILES, 2):
+                pack_two_tiles(
+                    nc, pack_banks, ident[:], x_sb[:, rt, :], x_sb[:, rt + 1, :],
+                    x_grouped[:, rt * P : (rt + 2) * P, :],
+                )
+            x_codes = once.tile([P, ROWS], U32, align_bytes=64)
+            x_scales = once.tile([P, ROWS], U8, align_bytes=64)
+            nc.vector.quantize_mx(
+                out=x_codes[:].bitcast(FP8X4),
+                scales=x_scales[:],
+                in_=x_grouped[:].rearrange("p r t -> p (r t)"),
+            )
+
+            pos_sq = once.tile([P, GROUPS * PACK], F32)
+            half_pos_sq = once.tile([P, GROUPS * PACK], F32)
+
+            def prepare_positions(g, pos):
+                cols = slice(g * PACK, (g + 1) * PACK)
+                for t in range(PACK):
+                    squares = stage.tile([P, FEATURES], BF16, tag="squares")
+                    nc.scalar.activation(
+                        out=squares[:], in_=pos[:, t, :], func=ACT.Square,
+                        accum_out=pos_sq[:, g * PACK + t : g * PACK + t + 1],
+                    )
+                nc.vector.tensor_scalar_mul(out=half_pos_sq[:, cols], in0=pos_sq[:, cols], scalar1=0.5)
+                grouped = stage.tile([P, K_PASS, PACK], BF16, tag="pos_grouped", align_bytes=64)
+                for t in range(0, PACK, 2):
+                    pack_two_tiles(
+                        nc, pack_banks, ident[:], pos[:, t, :], pos[:, t + 1, :],
+                        grouped[:, t * P : (t + 2) * P, :],
+                    )
+                codes = stage.tile([P, K_PASS], U32, tag="pos_codes", align_bytes=64)
+                scales = stage.tile([P, K_PASS], U8, tag="pos_scales", align_bytes=64)
+                nc.vector.quantize_mx(
+                    out=codes[:].bitcast(FP8X4),
+                    scales=scales[:],
+                    in_=grouped[:].rearrange("p c t -> p (c t)"),
+                )
+                return codes, scales
+
+            def distances(g, codes, scales):
+                y_tiles = []
+                for t in range(PACK):
+                    anchor = g * PACK + t
+                    y = y_pool.tile([P, ROWS], F32, tag="y")
+                    for half in range(ROW_HALVES):
+                        rows = slice(half * BANK, (half + 1) * BANK)
+                        dot = dot_banks.tile([P, BANK], F32, tag="dot")
+                        nc.tensor.matmul_mx(
+                            out=dot[:],
+                            lhsT=codes[:, t * P : (t + 1) * P].bitcast(FP8X4),
+                            lhsT_scale=scales[:, t * P : (t + 1) * P],
+                            rhs=x_codes[:, rows].bitcast(FP8X4),
+                            rhs_scale=x_scales[:, rows],
+                            start=True,
+                            stop=True,
+                        )
+                        nc.vector.scalar_tensor_tensor(
+                            out=y[:, rows],
+                            in0=half_x_sq_all[:, rows],
+                            scalar=half_pos_sq[:, anchor : anchor + 1],
+                            in1=dot[:],
+                            op0=ALU.add,
+                            op1=ALU.subtract,
+                        )
+                    y_tiles.append(y)
+                for t in range(PACK):
+                    anchor = g * PACK + t
+                    nc.vector.tensor_scalar(
+                        out=y_tiles[t][:],
+                        in0=y_tiles[t][:],
+                        scalar1=0.0,
+                        scalar2=two_over_tau_sq[:, anchor : anchor + 1],
+                        op0=ALU.max,
+                        op1=ALU.mult,
+                    )
+                for rt in range(ROW_TILES):
+                    turned = turn_banks.tile([P, PACK, P], F32, tag="turned")
+                    for t in range(PACK):
+                        nc.tensor.transpose(
+                            turned[:, t, :], y_tiles[t][:, rt * P : (rt + 1) * P], ident[:]
+                        )
+                    nc.scalar.activation(
+                        out=z[rt][:, g * K_PASS : (g + 1) * K_PASS],
+                        in_=turned[:].rearrange("p t c -> p (t c)"),
+                        func=ACT.Sqrt,
+                    )
+
+            operands = prepare_positions(0, pos_tiles[0])
+            for g in range(GROUPS):
+                this_group = operands
+                if g + 1 < GROUPS:
+                    operands = prepare_positions(g + 1, pos_tiles[g + 1])
+                if g + 3 < GROUPS:
+                    pos_tiles.append(load_positions(g + 3))
+                distances(g, this_group[0], this_group[1])
+
+            nc.sync.dma_start(
+                out=v_words[:].bitcast(I32),
+                in_=values_words.rearrange("g p n t -> p g (n t)").bitcast(I32),
+            )
+            for quadrant in range(4):
+                nc.sync.dma_start(
+                    out=v_scales[32 * quadrant : 32 * quadrant + 4, :, :].bitcast(I32),
+                    in_=values_scales[:, 4 * quadrant : 4 * quadrant + 4, :]
+                    .rearrange("g q n -> q g n")
+                    .bitcast(I32),
+                )
+
+        with ExitStack() as second:
+            small = second.enter_context(tc.tile_pool(name="small", bufs=2))
+            w_pool = second.enter_context(tc.tile_pool(name="w_pool", bufs=2))
+            out_pool = second.enter_context(tc.tile_pool(name="out_pool", bufs=3))
+            back_banks = second.enter_context(tc.psum_pool(name="back_banks", bufs=5))
+            spread_banks = second.enter_context(tc.psum_pool(name="spread_banks", bufs=1))
+            out_banks = second.enter_context(tc.psum_pool(name="out_banks", bufs=2))
+
+            def exponentials(rt):
+                nc.scalar.activation(
+                    out=z[rt][:], in_=z[rt][:], func=ACT.Exp, scale=-1.0,
+                    accum_out=row_sum[:, rt : rt + 1],
+                )
+
+            def weigh_values(rt):
+                inverse = small.tile([P, 1], F32, tag="inverse")
+                nc.vector.tensor_scalar_add(out=inverse[:], in0=row_sum[:, rt : rt + 1], scalar1=1e-8)
+                nc.vector.reciprocal(out=inverse[:], in_=inverse[:])
+                spread = spread_banks.tile([P, P], F32, tag="spread")
+                nc.tensor.transpose(spread[:], inverse[:].to_broadcast([P, P]), ident[:])
+                inverse_all = small.tile([P, P], F32, tag="inverse_all")
+                nc.scalar.copy(out=inverse_all[:], in_=spread[:])
+
+                w_grouped = w_pool.tile([P, GROUPS, P, PACK], BF16, tag="w_grouped", align_bytes=64)
+                for g in range(GROUPS):
+                    back = back_banks.tile([P, PACK, P], F32, tag="back")
+                    for t in range(PACK):
+                        first_col = g * K_PASS + t * P
+                        nc.tensor.transpose(back[:, t, :], z[rt][:, first_col : first_col + P], ident[:])
+                    nc.vector.tensor_tensor(
+                        out=w_grouped[:, g, :, :],
+                        in0=back[:].rearrange("p t r -> p r t"),
+                        in1=inverse_all[:].unsqueeze(2).to_broadcast([P, P, PACK]),
+                        op=ALU.mult,
+                    )
+                w_codes = w_pool.tile([P, GROUPS * P], U32, tag="w_codes", align_bytes=64)
+                w_scales = w_pool.tile([P, GROUPS * P], U8, tag="w_scales", align_bytes=64)
+                nc.vector.quantize_mx(
+                    out=w_codes[:].bitcast(FP8X4),
+                    scales=w_scales[:],
+                    in_=w_grouped[:].rearrange("p g r t -> p (g r t)"),
+                )
+                acc = out_banks.tile([P, FEATURES], F32, tag="acc")
+                for g in range(GROUPS):
+                    nc.tensor.matmul_mx(
+                        out=acc[:],
+                        lhsT=w_codes[:, g * P : (g + 1) * P].bitcast(FP8X4),
+                        lhsT_scale=w_scales[:, g * P : (g + 1) * P],
+                        rhs=v_words[:, g, :].bitcast(FP8X4),
+                        rhs_scale=v_scales[:, g, :],
+                        start=(g == 0),
+                        stop=(g == GROUPS - 1),
+                    )
+                result = out_pool.tile([P, FEATURES], F32, tag="result")
+                nc.scalar.copy(out=result[:], in_=acc[:])
+                nc.sync.dma_start(out=out_rows[rt * P : (rt + 1) * P, :], in_=result[:])
+
+            exponentials(0)
+            for rt in range(ROW_TILES):
+                if rt + 1 < ROW_TILES:
+                    exponentials(rt + 1)
+                weigh_values(rt)

@@ -22,20 +22,29 @@ ROW_TILES = ROWS // P
 GROUPS = ANCHORS // K_PASS
 BANK = 512
 ROW_HALVES = ROWS // BANK
+DOTS = PACK * ROW_HALVES
+RUN = 2
+PAIRS = GROUPS // 2
+AHEAD = 2
+LAG = PAIRS + AHEAD
 
 FLOPS = 2 * 2 * ROWS * ANCHORS * FEATURES
 
 
-def pack_two_tiles(nc, banks, ident, tile_a, tile_b, grouped):
-    bank = banks.tile([P, 2, 2, P], F32, tag="pack")
-    for a, tile in enumerate((tile_a, tile_b)):
-        words = tile.bitcast(F32)
-        for u in range(2):
-            nc.tensor.transpose(bank[:, a, u, :], words[:, u : FEATURES // 2 : 2], ident)
-    nc.scalar.copy(
-        out=grouped.bitcast(F32).rearrange("p (a c) u -> p a c u", a=2),
-        in_=bank[:].rearrange("p a u c -> p a c u"),
-    )
+def every_second_word(tile_a, tile_b):
+    words = (tile_a.bitcast(F32), tile_b.bitcast(F32))
+    return [words[a][:, u : FEATURES // 2 : 2] for a in range(2) for u in range(2)]
+
+
+def turn_words(nc, banks, ident, blocks):
+    bank = banks.tile([P, 2, 2, P], F32, tag="words")
+    for i, block in enumerate(blocks):
+        nc.tensor.transpose(bank[:, i // 2, i % 2, :], block, ident)
+    return bank
+
+
+def words_side_by_side(copy, bank, grouped):
+    copy(out=grouped.bitcast(F32), in_=bank[:].rearrange("p a u c -> p a c u"))
 
 
 def tile_multiscalegeometricattention_kernel(
@@ -46,13 +55,15 @@ def tile_multiscalegeometricattention_kernel(
     out_rows = out.flatten_outer_dims()
 
     with ExitStack() as whole:
+        whole.enter_context(tc.manual_schedule())
         keep = whole.enter_context(tc.tile_pool(name="keep", bufs=1))
 
         ident = keep.tile([P, P], F32)
         make_identity(nc, ident[:])
 
         z = [keep.tile([P, ANCHORS], F32, name="z%d" % rt) for rt in range(ROW_TILES)]
-        row_sum = keep.tile([P, ROW_TILES], F32)
+        row_sum = keep.tile([P, ROW_TILES, 2], F32)
+        inverse = keep.tile([P, ROW_TILES], F32)
 
         v_words = keep.tile([P, GROUPS, FEATURES], U32, align_bytes=64)
         v_scales = keep.tile([P, GROUPS, FEATURES], U8, align_bytes=64)
@@ -62,10 +73,13 @@ def tile_multiscalegeometricattention_kernel(
             once = first.enter_context(tc.tile_pool(name="once", bufs=1))
             loads = first.enter_context(tc.tile_pool(name="loads", bufs=3))
             stage = first.enter_context(tc.tile_pool(name="stage", bufs=2))
-            y_pool = first.enter_context(tc.tile_pool(name="y_pool", bufs=6))
-            pack_banks = first.enter_context(tc.psum_pool(name="pack_banks", bufs=2))
+            word_banks = first.enter_context(tc.psum_pool(name="word_banks", bufs=2))
             dot_banks = first.enter_context(tc.psum_pool(name="dot_banks", bufs=3))
             turn_banks = first.enter_context(tc.psum_pool(name="turn_banks", bufs=3))
+
+            warm = once.tile([P, 1], F32)
+            nc.vector.memset(warm[:], 1.0)
+            nc.scalar.activation(out=warm[:], in_=warm[:], func=ACT.Sqrt)
 
             def load_positions(g):
                 pos = loads.tile([P, PACK, FEATURES], BF16, tag="pos")
@@ -77,13 +91,91 @@ def tile_multiscalegeometricattention_kernel(
                 )
                 return pos
 
-            x_sb = once.tile([P, ROW_TILES, FEATURES], BF16)
-            nc.sync.dma_start(out=x_sb[:], in_=x_rows.rearrange("(rt p) d -> p rt d", p=P))
+            x_sq = once.tile([P, ROW_TILES], F32)
+            half_x_sq = once.tile([P, ROW_TILES], F32)
+            half_x_sq_all = once.tile([P, ROWS], F32)
+            x_codes = once.tile([P, ROWS], U32, align_bytes=64)
+            x_scales = once.tile([P, ROWS], U8, align_bytes=64)
             temp = once.tile([P, GROUPS, PACK], BF16)
-            nc.sync.dma_start(
-                out=temp[:], in_=temperature.rearrange("(g p t) -> p g t", p=P, t=PACK)
-            )
-            pos_tiles = [load_positions(g) for g in range(3)]
+            pos_sq = once.tile([P, GROUPS * PACK], F32)
+            half_pos_sq = once.tile([P, GROUPS * PACK], F32)
+            pos_tiles = []
+            grouped_tiles = []
+            operands = []
+
+            def square_positions(g, t):
+                squares = stage.tile([P, FEATURES], BF16, tag="squares")
+                nc.scalar.activation(
+                    out=squares[:], in_=pos_tiles[g][:, t, :], func=ACT.Square,
+                    accum_out=pos_sq[:, g * PACK + t : g * PACK + t + 1],
+                )
+
+            def pack_positions(g, pair, copy):
+                if pair == 0:
+                    grouped = stage.tile([P, PACK, P, PACK], BF16, tag="pos_grouped", align_bytes=64)
+                    grouped_tiles.append(grouped)
+                pos = pos_tiles[g]
+                bank = turn_words(
+                    nc, word_banks, ident[:],
+                    every_second_word(pos[:, 2 * pair, :], pos[:, 2 * pair + 1, :]),
+                )
+                words_side_by_side(copy, bank, grouped_tiles[g][:, 2 * pair : 2 * pair + 2, :, :])
+
+            def finish_positions(g):
+                codes = stage.tile([P, K_PASS], U32, tag="pos_codes", align_bytes=64)
+                scales = stage.tile([P, K_PASS], U8, tag="pos_scales", align_bytes=64)
+                nc.vector.quantize_mx(
+                    out=codes[:].bitcast(FP8X4),
+                    scales=scales[:],
+                    in_=grouped_tiles[g][:].rearrange("p a c t -> p (a c t)"),
+                )
+                operands.append((codes, scales))
+                cols = slice(g * PACK, (g + 1) * PACK)
+                nc.vector.tensor_scalar_mul(out=half_pos_sq[:, cols], in0=pos_sq[:, cols], scalar1=0.5)
+
+            with tc.tile_pool(name="x_pool", bufs=1) as x_pool:
+                x_sb = x_pool.tile([P, ROW_TILES, FEATURES], BF16)
+                for rt in range(0, ROW_TILES, 2):
+                    nc.sync.dma_start(
+                        out=x_sb[:, rt : rt + 2, :],
+                        in_=x_rows[rt * P : (rt + 2) * P, :].rearrange("(a p) d -> p a d", p=P),
+                    )
+                pos_tiles.append(load_positions(0))
+                nc.sync.dma_start(
+                    out=temp[:], in_=temperature.rearrange("(g p t) -> p g t", p=P, t=PACK)
+                )
+                pos_tiles.append(load_positions(1))
+                pos_tiles.append(load_positions(2))
+
+                x_grouped = x_pool.tile([P, ROW_TILES, P, PACK], BF16, align_bytes=64)
+                for rt in range(0, ROW_TILES, 2):
+                    bank = turn_words(
+                        nc, word_banks, ident[:],
+                        every_second_word(x_sb[:, rt, :], x_sb[:, rt + 1, :]),
+                    )
+                    words_side_by_side(nc.vector.tensor_copy, bank, x_grouped[:, rt : rt + 2, :, :])
+                    squares = stage.tile([P, 2, FEATURES], BF16, tag="x_squares")
+                    for a in range(2):
+                        nc.scalar.activation(
+                            out=squares[:, a, :], in_=x_sb[:, rt + a, :], func=ACT.Square,
+                            accum_out=x_sq[:, rt + a : rt + a + 1],
+                        )
+                tiles_in_half = ROW_TILES // ROW_HALVES
+                for half in range(ROW_HALVES):
+                    nc.vector.quantize_mx(
+                        out=x_codes[:, half * BANK : (half + 1) * BANK].bitcast(FP8X4),
+                        scales=x_scales[:, half * BANK : (half + 1) * BANK],
+                        in_=x_grouped[:, half * tiles_in_half : (half + 1) * tiles_in_half, :, :]
+                        .rearrange("p a c t -> p (a c t)"),
+                    )
+
+            y_pool = first.enter_context(tc.tile_pool(name="y_pool", bufs=2 * PACK))
+
+            for t in range(PACK):
+                square_positions(0, t)
+            for pair in range(PACK // 2):
+                pack_positions(0, pair, nc.vector.tensor_copy)
+            finish_positions(0)
 
             temp_flat = temp[:].rearrange("p g t -> p (g t)")
             tau = once.tile([P, GROUPS * PACK], F32)
@@ -100,18 +192,9 @@ def tile_multiscalegeometricattention_kernel(
             two_over_tau_sq = once.tile([P, GROUPS * PACK], F32)
             nc.vector.reciprocal(out=two_over_tau_sq[:], in_=half_tau_sq[:])
 
-            x_sq = once.tile([P, ROW_TILES], F32)
-            for rt in range(ROW_TILES):
-                squares = stage.tile([P, FEATURES], BF16, tag="squares")
-                nc.scalar.activation(
-                    out=squares[:], in_=x_sb[:, rt, :], func=ACT.Square,
-                    accum_out=x_sq[:, rt : rt + 1],
-                )
-            half_x_sq = once.tile([P, ROW_TILES], F32)
             nc.vector.tensor_scalar_mul(out=half_x_sq[:], in0=x_sq[:], scalar1=0.5)
-            half_x_sq_all = once.tile([P, ROWS], F32)
             for half in range(ROW_HALVES):
-                spread = pack_banks.tile([P, BANK], F32, tag="pack")
+                spread = word_banks.tile([P, BANK], F32, tag="words")
                 for i in range(BANK // P):
                     rt = half * (BANK // P) + i
                     nc.tensor.transpose(
@@ -119,105 +202,84 @@ def tile_multiscalegeometricattention_kernel(
                         half_x_sq[:, rt : rt + 1].to_broadcast([P, P]),
                         ident[:],
                     )
-                nc.scalar.copy(out=half_x_sq_all[:, half * BANK : (half + 1) * BANK], in_=spread[:])
-
-            x_grouped = once.tile([P, ROWS, PACK], BF16, align_bytes=64)
-            for rt in range(0, ROW_TILES, 2):
-                pack_two_tiles(
-                    nc, pack_banks, ident[:], x_sb[:, rt, :], x_sb[:, rt + 1, :],
-                    x_grouped[:, rt * P : (rt + 2) * P, :],
+                nc.vector.tensor_copy(
+                    out=half_x_sq_all[:, half * BANK : (half + 1) * BANK], in_=spread[:]
                 )
-            x_codes = once.tile([P, ROWS], U32, align_bytes=64)
-            x_scales = once.tile([P, ROWS], U8, align_bytes=64)
-            nc.vector.quantize_mx(
-                out=x_codes[:].bitcast(FP8X4),
-                scales=x_scales[:],
-                in_=x_grouped[:].rearrange("p r t -> p (r t)"),
-            )
 
-            pos_sq = once.tile([P, GROUPS * PACK], F32)
-            half_pos_sq = once.tile([P, GROUPS * PACK], F32)
+            y_tiles = []
 
-            def prepare_positions(g, pos):
-                cols = slice(g * PACK, (g + 1) * PACK)
-                for t in range(PACK):
-                    squares = stage.tile([P, FEATURES], BF16, tag="squares")
-                    nc.scalar.activation(
-                        out=squares[:], in_=pos[:, t, :], func=ACT.Square,
-                        accum_out=pos_sq[:, g * PACK + t : g * PACK + t + 1],
-                    )
-                nc.vector.tensor_scalar_mul(out=half_pos_sq[:, cols], in0=pos_sq[:, cols], scalar1=0.5)
-                grouped = stage.tile([P, K_PASS, PACK], BF16, tag="pos_grouped", align_bytes=64)
-                for t in range(0, PACK, 2):
-                    pack_two_tiles(
-                        nc, pack_banks, ident[:], pos[:, t, :], pos[:, t + 1, :],
-                        grouped[:, t * P : (t + 2) * P, :],
-                    )
-                codes = stage.tile([P, K_PASS], U32, tag="pos_codes", align_bytes=64)
-                scales = stage.tile([P, K_PASS], U8, tag="pos_scales", align_bytes=64)
-                nc.vector.quantize_mx(
-                    out=codes[:].bitcast(FP8X4),
-                    scales=scales[:],
-                    in_=grouped[:].rearrange("p c t -> p (c t)"),
-                )
-                return codes, scales
-
-            def distances(g, codes, scales):
-                y_tiles = []
-                for t in range(PACK):
-                    anchor = g * PACK + t
+            def dot_products(g, j):
+                t, half = j // ROW_HALVES, j % ROW_HALVES
+                if half == 0:
                     y = y_pool.tile([P, ROWS], F32, tag="y")
-                    for half in range(ROW_HALVES):
-                        rows = slice(half * BANK, (half + 1) * BANK)
-                        dot = dot_banks.tile([P, BANK], F32, tag="dot")
-                        nc.tensor.matmul_mx(
-                            out=dot[:],
-                            lhsT=codes[:, t * P : (t + 1) * P].bitcast(FP8X4),
-                            lhsT_scale=scales[:, t * P : (t + 1) * P],
-                            rhs=x_codes[:, rows].bitcast(FP8X4),
-                            rhs_scale=x_scales[:, rows],
-                            start=True,
-                            stop=True,
-                        )
-                        nc.vector.scalar_tensor_tensor(
-                            out=y[:, rows],
-                            in0=half_x_sq_all[:, rows],
-                            scalar=half_pos_sq[:, anchor : anchor + 1],
-                            in1=dot[:],
-                            op0=ALU.add,
-                            op1=ALU.subtract,
-                        )
                     y_tiles.append(y)
-                for t in range(PACK):
-                    anchor = g * PACK + t
-                    nc.vector.tensor_scalar(
-                        out=y_tiles[t][:],
-                        in0=y_tiles[t][:],
-                        scalar1=0.0,
-                        scalar2=two_over_tau_sq[:, anchor : anchor + 1],
-                        op0=ALU.max,
-                        op1=ALU.mult,
-                    )
-                for rt in range(ROW_TILES):
-                    turned = turn_banks.tile([P, PACK, P], F32, tag="turned")
-                    for t in range(PACK):
-                        nc.tensor.transpose(
-                            turned[:, t, :], y_tiles[t][:, rt * P : (rt + 1) * P], ident[:]
-                        )
-                    nc.scalar.activation(
-                        out=z[rt][:, g * K_PASS : (g + 1) * K_PASS],
-                        in_=turned[:].rearrange("p t c -> p (t c)"),
-                        func=ACT.Sqrt,
-                    )
+                codes, scales = operands[g]
+                anchor = g * PACK + t
+                rows = slice(half * BANK, (half + 1) * BANK)
+                dot = dot_banks.tile([P, BANK], F32, tag="dot")
+                nc.tensor.matmul_mx(
+                    out=dot[:],
+                    lhsT=codes[:, t * P : (t + 1) * P].bitcast(FP8X4),
+                    lhsT_scale=scales[:, t * P : (t + 1) * P],
+                    rhs=x_codes[:, rows].bitcast(FP8X4),
+                    rhs_scale=x_scales[:, rows],
+                    start=True,
+                    stop=True,
+                )
+                nc.vector.scalar_tensor_tensor(
+                    out=y_tiles[anchor][:, rows],
+                    in0=half_x_sq_all[:, rows],
+                    scalar=half_pos_sq[:, anchor : anchor + 1],
+                    in1=dot[:],
+                    op0=ALU.add,
+                    op1=ALU.subtract,
+                )
 
-            operands = prepare_positions(0, pos_tiles[0])
-            for g in range(GROUPS):
-                this_group = operands
-                if g + 1 < GROUPS:
-                    operands = prepare_positions(g + 1, pos_tiles[g + 1])
-                if g + 3 < GROUPS:
-                    pos_tiles.append(load_positions(g + 3))
-                distances(g, this_group[0], this_group[1])
+            def clamp_and_scale(g, t):
+                anchor = g * PACK + t
+                nc.vector.tensor_scalar(
+                    out=y_tiles[anchor][:],
+                    in0=y_tiles[anchor][:],
+                    scalar1=0.0,
+                    scalar2=two_over_tau_sq[:, anchor : anchor + 1],
+                    op0=ALU.max,
+                    op1=ALU.mult,
+                )
+
+            def turn_and_root(g, rt):
+                turned = turn_banks.tile([P, PACK, P], F32, tag="turned")
+                for t in range(PACK):
+                    nc.tensor.transpose(
+                        turned[:, t, :], y_tiles[g * PACK + t][:, rt * P : (rt + 1) * P], ident[:]
+                    )
+                nc.scalar.activation(
+                    out=z[rt][:, g * K_PASS : (g + 1) * K_PASS].rearrange(
+                        "r (u p e) -> r u p e", u=2, e=2
+                    ),
+                    in_=turned[:].rearrange("r (u e) p -> r u p e", e=2),
+                    func=ACT.Sqrt,
+                )
+
+            for s in range(GROUPS + 1):
+                for first_j in range(0, DOTS, RUN):
+                    for j in range(first_j, first_j + RUN):
+                        if s < GROUPS:
+                            dot_products(s, j)
+                            if j >= ROW_HALVES and j % ROW_HALVES == 0:
+                                clamp_and_scale(s, j // ROW_HALVES - 1)
+                    for j in range(first_j, first_j + RUN):
+                        if s >= 1:
+                            turn_and_root(s - 1, j)
+                        if s + 1 < GROUPS and j < PACK:
+                            square_positions(s + 1, j)
+                        if s + 1 < GROUPS and j < PACK // 2:
+                            pack_positions(s + 1, j, nc.scalar.copy)
+                if s + 1 < GROUPS:
+                    finish_positions(s + 1)
+                if s < GROUPS:
+                    clamp_and_scale(s, PACK - 1)
+                if s + 3 < GROUPS:
+                    pos_tiles.append(load_positions(s + 3))
 
             nc.sync.dma_start(
                 out=v_words[:].bitcast(I32),
@@ -232,51 +294,71 @@ def tile_multiscalegeometricattention_kernel(
                 )
 
         with ExitStack() as second:
-            small = second.enter_context(tc.tile_pool(name="small", bufs=2))
             w_pool = second.enter_context(tc.tile_pool(name="w_pool", bufs=2))
             out_pool = second.enter_context(tc.tile_pool(name="out_pool", bufs=3))
-            back_banks = second.enter_context(tc.psum_pool(name="back_banks", bufs=5))
-            spread_banks = second.enter_context(tc.psum_pool(name="spread_banks", bufs=1))
+            back_banks = second.enter_context(tc.psum_pool(name="back_banks", bufs=6))
             out_banks = second.enter_context(tc.psum_pool(name="out_banks", bufs=2))
 
+            w_tiles = []
+            w_grouped_tiles = []
+            w_operands = []
+            banks = []
+            acc_tiles = []
+            half_row = ANCHORS // 2
+
             def exponentials(rt):
-                nc.scalar.activation(
-                    out=z[rt][:], in_=z[rt][:], func=ACT.Exp, scale=-1.0,
-                    accum_out=row_sum[:, rt : rt + 1],
-                )
-
-            def weigh_values(rt):
-                inverse = small.tile([P, 1], F32, tag="inverse")
-                nc.vector.tensor_scalar_add(out=inverse[:], in0=row_sum[:, rt : rt + 1], scalar1=1e-8)
-                nc.vector.reciprocal(out=inverse[:], in_=inverse[:])
-                spread = spread_banks.tile([P, P], F32, tag="spread")
-                nc.tensor.transpose(spread[:], inverse[:].to_broadcast([P, P]), ident[:])
-                inverse_all = small.tile([P, P], F32, tag="inverse_all")
-                nc.scalar.copy(out=inverse_all[:], in_=spread[:])
-
-                w_grouped = w_pool.tile([P, GROUPS, P, PACK], BF16, tag="w_grouped", align_bytes=64)
-                for g in range(GROUPS):
-                    back = back_banks.tile([P, PACK, P], F32, tag="back")
-                    for t in range(PACK):
-                        first_col = g * K_PASS + t * P
-                        nc.tensor.transpose(back[:, t, :], z[rt][:, first_col : first_col + P], ident[:])
-                    nc.vector.tensor_tensor(
-                        out=w_grouped[:, g, :, :],
-                        in0=back[:].rearrange("p t r -> p r t"),
-                        in1=inverse_all[:].unsqueeze(2).to_broadcast([P, P, PACK]),
-                        op=ALU.mult,
+                for h in range(2):
+                    cols = slice(h * half_row, (h + 1) * half_row)
+                    nc.scalar.activation(
+                        out=z[rt][:, cols], in_=z[rt][:, cols], func=ACT.Exp, scale=-1.0,
+                        accum_out=row_sum[:, rt, h : h + 1],
                     )
-                w_codes = w_pool.tile([P, GROUPS * P], U32, tag="w_codes", align_bytes=64)
-                w_scales = w_pool.tile([P, GROUPS * P], U8, tag="w_scales", align_bytes=64)
-                nc.vector.quantize_mx(
-                    out=w_codes[:].bitcast(FP8X4),
-                    scales=w_scales[:],
-                    in_=w_grouped[:].rearrange("p g r t -> p (g r t)"),
+
+            def normalise(rt, pair):
+                if pair == 0:
+                    nc.vector.scalar_tensor_tensor(
+                        out=inverse[:, rt : rt + 1], in0=row_sum[:, rt, 0:1], scalar=1e-8,
+                        in1=row_sum[:, rt, 1:2], op0=ALU.add, op1=ALU.add,
+                    )
+                    nc.vector.reciprocal(out=inverse[:, rt : rt + 1], in_=inverse[:, rt : rt + 1])
+                    w = w_pool.tile([P, ANCHORS], BF16, tag="w")
+                    w_tiles.append(w)
+                cols = slice(pair * 2 * K_PASS, (pair + 1) * 2 * K_PASS)
+                nc.vector.tensor_scalar_mul(
+                    out=w_tiles[rt][:, cols], in0=z[rt][:, cols], scalar1=inverse[:, rt : rt + 1]
                 )
-                acc = out_banks.tile([P, FEATURES], F32, tag="acc")
-                for g in range(GROUPS):
+
+            def turn_back(rt, pair):
+                words = w_tiles[rt][:].bitcast(F32)
+                blocks = [words[:, (4 * pair + i) * P : (4 * pair + i + 1) * P] for i in range(4)]
+                banks.append(turn_words(nc, back_banks, ident[:], blocks))
+
+            def copy_out(rt, pair):
+                if pair == 0:
+                    w_grouped = w_pool.tile([P, GROUPS, P, PACK], BF16, tag="w_grouped", align_bytes=64)
+                    w_grouped_tiles.append(w_grouped)
+                words_side_by_side(
+                    nc.vector.tensor_copy, banks[rt * PAIRS + pair],
+                    w_grouped_tiles[rt][:, 2 * pair : 2 * pair + 2, :, :],
+                )
+                if pair == PAIRS - 1:
+                    w_codes = w_pool.tile([P, GROUPS * P], U32, tag="w_codes", align_bytes=64)
+                    w_scales = w_pool.tile([P, GROUPS * P], U8, tag="w_scales", align_bytes=64)
+                    nc.vector.quantize_mx(
+                        out=w_codes[:].bitcast(FP8X4),
+                        scales=w_scales[:],
+                        in_=w_grouped_tiles[rt][:].rearrange("p g r t -> p (g r t)"),
+                    )
+                    w_operands.append((w_codes, w_scales))
+
+            def weigh_values(rt, pair):
+                if pair == 0:
+                    acc = out_banks.tile([P, FEATURES], F32, tag="acc")
+                    acc_tiles.append(acc)
+                w_codes, w_scales = w_operands[rt]
+                for g in range(2 * pair, 2 * pair + 2):
                     nc.tensor.matmul_mx(
-                        out=acc[:],
+                        out=acc_tiles[rt][:],
                         lhsT=w_codes[:, g * P : (g + 1) * P].bitcast(FP8X4),
                         lhsT_scale=w_scales[:, g * P : (g + 1) * P],
                         rhs=v_words[:, g, :].bitcast(FP8X4),
@@ -284,12 +366,21 @@ def tile_multiscalegeometricattention_kernel(
                         start=(g == 0),
                         stop=(g == GROUPS - 1),
                     )
-                result = out_pool.tile([P, FEATURES], F32, tag="result")
-                nc.scalar.copy(out=result[:], in_=acc[:])
-                nc.sync.dma_start(out=out_rows[rt * P : (rt + 1) * P, :], in_=result[:])
+                if pair == PAIRS - 1:
+                    result = out_pool.tile([P, FEATURES], F32, tag="result")
+                    nc.scalar.copy(out=result[:], in_=acc_tiles[rt][:])
+                    nc.sync.dma_start(out=out_rows[rt * P : (rt + 1) * P, :], in_=result[:])
 
             exponentials(0)
-            for rt in range(ROW_TILES):
-                if rt + 1 < ROW_TILES:
-                    exponentials(rt + 1)
-                weigh_values(rt)
+            exponentials(1)
+            all_banks = ROW_TILES * PAIRS
+            for b in range(all_banks + LAG):
+                if b % PAIRS == 0 and b // PAIRS + 2 < ROW_TILES:
+                    exponentials(b // PAIRS + 2)
+                if b < all_banks:
+                    normalise(b // PAIRS, b % PAIRS)
+                    turn_back(b // PAIRS, b % PAIRS)
+                if AHEAD <= b < all_banks + AHEAD:
+                    copy_out((b - AHEAD) // PAIRS, (b - AHEAD) % PAIRS)
+                if b >= LAG:
+                    weigh_values((b - LAG) // PAIRS, (b - LAG) % PAIRS)

@@ -171,11 +171,12 @@ def tile_multiscalegeometricattention_kernel(
 
             y_pool = first.enter_context(tc.tile_pool(name="y_pool", bufs=2 * PACK))
 
-            for t in range(PACK):
-                square_positions(0, t)
-            for pair in range(PACK // 2):
-                pack_positions(0, pair, nc.vector.tensor_copy)
-            finish_positions(0)
+            for g in range(2):
+                for t in range(PACK):
+                    square_positions(g, t)
+                for pair in range(PACK // 2):
+                    pack_positions(g, pair, nc.vector.tensor_copy)
+                pos_tiles.append(load_positions(g + 3))
 
             temp_flat = temp[:].rearrange("p g t -> p (g t)")
             tau = once.tile([P, GROUPS * PACK], F32)
@@ -205,6 +206,7 @@ def tile_multiscalegeometricattention_kernel(
                 nc.vector.tensor_copy(
                     out=half_x_sq_all[:, half * BANK : (half + 1) * BANK], in_=spread[:]
                 )
+            finish_positions(0)
 
             y_tiles = []
 
@@ -267,19 +269,19 @@ def tile_multiscalegeometricattention_kernel(
                             dot_products(s, j)
                             if j >= ROW_HALVES and j % ROW_HALVES == 0:
                                 clamp_and_scale(s, j // ROW_HALVES - 1)
+                    if first_j == DOTS // 2 and s + 1 < GROUPS:
+                        finish_positions(s + 1)
                     for j in range(first_j, first_j + RUN):
                         if s >= 1:
                             turn_and_root(s - 1, j)
-                        if s + 1 < GROUPS and j < PACK:
-                            square_positions(s + 1, j)
-                        if s + 1 < GROUPS and j < PACK // 2:
-                            pack_positions(s + 1, j, nc.scalar.copy)
-                if s + 1 < GROUPS:
-                    finish_positions(s + 1)
+                        if s + 2 < GROUPS and j % 2 == 0:
+                            square_positions(s + 2, j // 2)
+                        if s + 2 < GROUPS and j % 4 == 1:
+                            pack_positions(s + 2, j // 4, nc.scalar.copy)
                 if s < GROUPS:
                     clamp_and_scale(s, PACK - 1)
-                if s + 3 < GROUPS:
-                    pos_tiles.append(load_positions(s + 3))
+                if s + 5 < GROUPS:
+                    pos_tiles.append(load_positions(s + 5))
 
             nc.sync.dma_start(
                 out=v_words[:].bitcast(I32),
@@ -337,8 +339,9 @@ def tile_multiscalegeometricattention_kernel(
                 if pair == 0:
                     w_grouped = w_pool.tile([P, GROUPS, P, PACK], BF16, tag="w_grouped", align_bytes=64)
                     w_grouped_tiles.append(w_grouped)
+                copy = nc.scalar.copy if pair == 1 else nc.vector.tensor_copy
                 words_side_by_side(
-                    nc.vector.tensor_copy, banks[rt * PAIRS + pair],
+                    copy, banks[rt * PAIRS + pair],
                     w_grouped_tiles[rt][:, 2 * pair : 2 * pair + 2, :, :],
                 )
                 if pair == PAIRS - 1:

@@ -24,9 +24,11 @@ BANK = 512
 ROW_HALVES = ROWS // BANK
 DOTS = PACK * ROW_HALVES
 RUN = 2
+TURN_LAG = DOTS + RUN
+EXP_AHEAD = 2
 PAIRS = GROUPS // 2
 AHEAD = 2
-LAG = PAIRS + AHEAD
+LAG = AHEAD + 2
 
 FLOPS = 2 * 2 * ROWS * ANCHORS * FEATURES
 
@@ -62,7 +64,8 @@ def tile_multiscalegeometricattention_kernel(
         make_identity(nc, ident[:])
 
         z = [keep.tile([P, ANCHORS], F32, name="z%d" % rt) for rt in range(ROW_TILES)]
-        row_sum = keep.tile([P, ROW_TILES, 2], F32)
+        part_sum = keep.tile([P, ROW_TILES, PAIRS], F32)
+        row_sum = keep.tile([P, ROW_TILES], F32)
         inverse = keep.tile([P, ROW_TILES], F32)
 
         v_words = keep.tile([P, GROUPS, FEATURES], U32, align_bytes=64)
@@ -154,7 +157,7 @@ def tile_multiscalegeometricattention_kernel(
                         every_second_word(x_sb[:, rt, :], x_sb[:, rt + 1, :]),
                     )
                     words_side_by_side(nc.vector.tensor_copy, bank, x_grouped[:, rt : rt + 2, :, :])
-                    squares = stage.tile([P, 2, FEATURES], BF16, tag="x_squares")
+                    squares = x_pool.tile([P, 2, FEATURES], BF16, tag="x_squares", bufs=2)
                     for a in range(2):
                         nc.scalar.activation(
                             out=squares[:, a, :], in_=x_sb[:, rt + a, :], func=ACT.Square,
@@ -169,7 +172,9 @@ def tile_multiscalegeometricattention_kernel(
                         .rearrange("p a c t -> p (a c t)"),
                     )
 
-            y_pool = first.enter_context(tc.tile_pool(name="y_pool", bufs=2 * PACK))
+            y_pool = first.enter_context(
+                tc.tile_pool(name="y_pool", bufs=(TURN_LAG + DOTS) // ROW_HALVES + 1)
+            )
 
             for g in range(2):
                 for t in range(PACK):
@@ -237,8 +242,7 @@ def tile_multiscalegeometricattention_kernel(
                     op1=ALU.subtract,
                 )
 
-            def clamp_and_scale(g, t):
-                anchor = g * PACK + t
+            def clamp_and_scale(anchor):
                 nc.vector.tensor_scalar(
                     out=y_tiles[anchor][:],
                     in0=y_tiles[anchor][:],
@@ -262,26 +266,26 @@ def tile_multiscalegeometricattention_kernel(
                     func=ACT.Sqrt,
                 )
 
-            for s in range(GROUPS + 1):
-                for first_j in range(0, DOTS, RUN):
-                    for j in range(first_j, first_j + RUN):
-                        if s < GROUPS:
-                            dot_products(s, j)
-                            if j >= ROW_HALVES and j % ROW_HALVES == 0:
-                                clamp_and_scale(s, j // ROW_HALVES - 1)
-                    if first_j == DOTS // 2 and s + 1 < GROUPS:
+            all_dots = GROUPS * DOTS
+            for first_unit in range(0, all_dots + TURN_LAG, RUN):
+                for unit in range(first_unit, first_unit + RUN):
+                    s, j = unit // DOTS, unit % DOTS
+                    if unit < all_dots:
+                        dot_products(s, j)
+                    if ROW_HALVES <= unit <= all_dots and unit % ROW_HALVES == 0:
+                        clamp_and_scale(unit // ROW_HALVES - 1)
+                    if j == DOTS // 2 and s + 1 < GROUPS:
                         finish_positions(s + 1)
-                    for j in range(first_j, first_j + RUN):
-                        if s >= 1:
-                            turn_and_root(s - 1, j)
-                        if s + 2 < GROUPS and j % 2 == 0:
-                            square_positions(s + 2, j // 2)
-                        if s + 2 < GROUPS and j % 4 == 1:
-                            pack_positions(s + 2, j // 4, nc.scalar.copy)
-                if s < GROUPS:
-                    clamp_and_scale(s, PACK - 1)
-                if s + 5 < GROUPS:
-                    pos_tiles.append(load_positions(s + 5))
+                for unit in range(first_unit, first_unit + RUN):
+                    s, j = unit // DOTS, unit % DOTS
+                    if unit >= TURN_LAG:
+                        turn_and_root((unit - TURN_LAG) // DOTS, (unit - TURN_LAG) % DOTS)
+                    if s + 2 < GROUPS and j % 2 == 0:
+                        square_positions(s + 2, j // 2)
+                    if s + 2 < GROUPS and j % 4 == 1:
+                        pack_positions(s + 2, j // 4, nc.scalar.copy)
+                    if s + 5 < GROUPS and j == DOTS - 1:
+                        pos_tiles.append(load_positions(s + 5))
 
             nc.sync.dma_start(
                 out=v_words[:].bitcast(I32),
@@ -306,28 +310,36 @@ def tile_multiscalegeometricattention_kernel(
             w_operands = []
             banks = []
             acc_tiles = []
-            half_row = ANCHORS // 2
 
-            def exponentials(rt):
-                for h in range(2):
-                    cols = slice(h * half_row, (h + 1) * half_row)
-                    nc.scalar.activation(
-                        out=z[rt][:, cols], in_=z[rt][:, cols], func=ACT.Exp, scale=-1.0,
-                        accum_out=row_sum[:, rt, h : h + 1],
-                    )
+            def two_groups(pair):
+                return slice(pair * 2 * K_PASS, (pair + 1) * 2 * K_PASS)
+
+            def exponentials(rt, pair):
+                nc.scalar.activation(
+                    out=z[rt][:, two_groups(pair)], in_=z[rt][:, two_groups(pair)], func=ACT.Exp,
+                    scale=-1.0, accum_out=part_sum[:, rt, pair : pair + 1],
+                )
+
+            def add_part_sums(rt):
+                nc.vector.reduce_sum(
+                    out=row_sum[:, rt : rt + 1], in_=part_sum[:, rt, :], axis=mybir.AxisListType.X
+                )
+
+            def add_epsilon(rt):
+                nc.vector.tensor_scalar_add(
+                    out=row_sum[:, rt : rt + 1], in0=row_sum[:, rt : rt + 1], scalar1=1e-8
+                )
+
+            def invert(rt):
+                nc.vector.reciprocal(out=inverse[:, rt : rt + 1], in_=row_sum[:, rt : rt + 1])
 
             def normalise(rt, pair):
                 if pair == 0:
-                    nc.vector.scalar_tensor_tensor(
-                        out=inverse[:, rt : rt + 1], in0=row_sum[:, rt, 0:1], scalar=1e-8,
-                        in1=row_sum[:, rt, 1:2], op0=ALU.add, op1=ALU.add,
-                    )
-                    nc.vector.reciprocal(out=inverse[:, rt : rt + 1], in_=inverse[:, rt : rt + 1])
                     w = w_pool.tile([P, ANCHORS], BF16, tag="w")
                     w_tiles.append(w)
-                cols = slice(pair * 2 * K_PASS, (pair + 1) * 2 * K_PASS)
                 nc.vector.tensor_scalar_mul(
-                    out=w_tiles[rt][:, cols], in0=z[rt][:, cols], scalar1=inverse[:, rt : rt + 1]
+                    out=w_tiles[rt][:, two_groups(pair)], in0=z[rt][:, two_groups(pair)],
+                    scalar1=inverse[:, rt : rt + 1],
                 )
 
             def turn_back(rt, pair):
@@ -339,20 +351,25 @@ def tile_multiscalegeometricattention_kernel(
                 if pair == 0:
                     w_grouped = w_pool.tile([P, GROUPS, P, PACK], BF16, tag="w_grouped", align_bytes=64)
                     w_grouped_tiles.append(w_grouped)
-                copy = nc.scalar.copy if pair == 1 else nc.vector.tensor_copy
+                    w_codes = w_pool.tile([P, GROUPS * P], U32, tag="w_codes", align_bytes=64)
+                    w_scales = w_pool.tile([P, GROUPS * P], U8, tag="w_scales", align_bytes=64)
+                    w_operands.append((w_codes, w_scales))
+                scalar_is_free = rt + EXP_AHEAD >= ROW_TILES
+                copy = nc.scalar.copy if scalar_is_free else nc.vector.tensor_copy
                 words_side_by_side(
                     copy, banks[rt * PAIRS + pair],
                     w_grouped_tiles[rt][:, 2 * pair : 2 * pair + 2, :, :],
                 )
-                if pair == PAIRS - 1:
-                    w_codes = w_pool.tile([P, GROUPS * P], U32, tag="w_codes", align_bytes=64)
-                    w_scales = w_pool.tile([P, GROUPS * P], U8, tag="w_scales", align_bytes=64)
+                if pair % 2 == 1:
+                    w_codes, w_scales = w_operands[rt]
+                    cols = slice((pair - 1) * 2 * P, (pair + 1) * 2 * P)
                     nc.vector.quantize_mx(
-                        out=w_codes[:].bitcast(FP8X4),
-                        scales=w_scales[:],
-                        in_=w_grouped_tiles[rt][:].rearrange("p g r t -> p (g r t)"),
+                        out=w_codes[:, cols].bitcast(FP8X4),
+                        scales=w_scales[:, cols],
+                        in_=w_grouped_tiles[rt][:, 2 * pair - 2 : 2 * pair + 2, :, :].rearrange(
+                            "p g r t -> p (g r t)"
+                        ),
                     )
-                    w_operands.append((w_codes, w_scales))
 
             def weigh_values(rt, pair):
                 if pair == 0:
@@ -374,16 +391,30 @@ def tile_multiscalegeometricattention_kernel(
                     nc.scalar.copy(out=result[:], in_=acc_tiles[rt][:])
                     nc.sync.dma_start(out=out_rows[rt * P : (rt + 1) * P, :], in_=result[:])
 
-            exponentials(0)
-            exponentials(1)
+            for pair in range(PAIRS):
+                exponentials(0, pair)
+            add_part_sums(0)
+            add_epsilon(0)
+            invert(0)
+            for rt in range(1, EXP_AHEAD):
+                for pair in range(PAIRS):
+                    exponentials(rt, pair)
             all_banks = ROW_TILES * PAIRS
             for b in range(all_banks + LAG):
-                if b % PAIRS == 0 and b // PAIRS + 2 < ROW_TILES:
-                    exponentials(b // PAIRS + 2)
+                rt, pair = b // PAIRS, b % PAIRS
+                next_sum = pair == PAIRS - 1 and rt + 1 < ROW_TILES
+                if rt + EXP_AHEAD < ROW_TILES:
+                    exponentials(rt + EXP_AHEAD, pair)
+                if next_sum:
+                    add_part_sums(rt + 1)
                 if b < all_banks:
-                    normalise(b // PAIRS, b % PAIRS)
-                    turn_back(b // PAIRS, b % PAIRS)
+                    normalise(rt, pair)
+                    turn_back(rt, pair)
+                if next_sum:
+                    add_epsilon(rt + 1)
                 if AHEAD <= b < all_banks + AHEAD:
                     copy_out((b - AHEAD) // PAIRS, (b - AHEAD) % PAIRS)
+                if next_sum:
+                    invert(rt + 1)
                 if b >= LAG:
                     weigh_values((b - LAG) // PAIRS, (b - LAG) % PAIRS)

@@ -28,7 +28,7 @@ TURN_LAG = DOTS + RUN
 EXP_AHEAD = 2
 PAIRS = GROUPS // 2
 AHEAD = 2
-LAG = AHEAD + 2
+LAG = AHEAD + 3
 
 FLOPS = 2 * 2 * ROWS * ANCHORS * FEATURES
 
@@ -360,16 +360,17 @@ def tile_multiscalegeometricattention_kernel(
                     copy, banks[rt * PAIRS + pair],
                     w_grouped_tiles[rt][:, 2 * pair : 2 * pair + 2, :, :],
                 )
-                if pair % 2 == 1:
-                    w_codes, w_scales = w_operands[rt]
-                    cols = slice((pair - 1) * 2 * P, (pair + 1) * 2 * P)
-                    nc.vector.quantize_mx(
-                        out=w_codes[:, cols].bitcast(FP8X4),
-                        scales=w_scales[:, cols],
-                        in_=w_grouped_tiles[rt][:, 2 * pair - 2 : 2 * pair + 2, :, :].rearrange(
-                            "p g r t -> p (g r t)"
-                        ),
-                    )
+
+            def quantise(rt, pair):
+                w_codes, w_scales = w_operands[rt]
+                cols = slice((pair - 1) * 2 * P, (pair + 1) * 2 * P)
+                nc.vector.quantize_mx(
+                    out=w_codes[:, cols].bitcast(FP8X4),
+                    scales=w_scales[:, cols],
+                    in_=w_grouped_tiles[rt][:, 2 * pair - 2 : 2 * pair + 2, :, :].rearrange(
+                        "p g r t -> p (g r t)"
+                    ),
+                )
 
             def weigh_values(rt, pair):
                 if pair == 0:
@@ -412,6 +413,9 @@ def tile_multiscalegeometricattention_kernel(
                     turn_back(rt, pair)
                 if next_sum:
                     add_epsilon(rt + 1)
+                copied = b - AHEAD - 1
+                if 0 <= copied < all_banks and copied % 2 == 1:
+                    quantise(copied // PAIRS, copied % PAIRS)
                 if AHEAD <= b < all_banks + AHEAD:
                     copy_out((b - AHEAD) // PAIRS, (b - AHEAD) % PAIRS)
                 if next_sum:

@@ -25,9 +25,10 @@ ROW_HALVES = ROWS // BANK
 DOTS = PACK * ROW_HALVES
 RUN = 2
 TURN_LAG = DOTS + RUN
-EXP_AHEAD = 2
+EXP_AHEAD = 3
 PAIRS = GROUPS // 2
 AHEAD = 2
+CATCH_UP_FROM = 56
 LAG = AHEAD + 3
 
 FLOPS = 2 * 2 * ROWS * ANCHORS * FEATURES
@@ -176,12 +177,25 @@ def tile_multiscalegeometricattention_kernel(
                 tc.tile_pool(name="y_pool", bufs=(TURN_LAG + DOTS) // ROW_HALVES + 1)
             )
 
-            for g in range(2):
-                for t in range(PACK):
-                    square_positions(g, t)
-                for pair in range(PACK // 2):
-                    pack_positions(g, pair, nc.vector.tensor_copy)
-                pos_tiles.append(load_positions(g + 3))
+            nc.vector.tensor_scalar_mul(out=half_x_sq[:], in0=x_sq[:], scalar1=0.5)
+            for t in range(PACK):
+                square_positions(0, t)
+            for pair in range(PACK // 2):
+                pack_positions(0, pair, nc.vector.tensor_copy)
+            pos_tiles.append(load_positions(3))
+
+            for half in range(ROW_HALVES):
+                spread = word_banks.tile([P, BANK], F32, tag="words")
+                for i in range(BANK // P):
+                    rt = half * (BANK // P) + i
+                    nc.tensor.transpose(
+                        spread[:, i * P : (i + 1) * P],
+                        half_x_sq[:, rt : rt + 1].to_broadcast([P, P]),
+                        ident[:],
+                    )
+                nc.vector.tensor_copy(
+                    out=half_x_sq_all[:, half * BANK : (half + 1) * BANK], in_=spread[:]
+                )
 
             temp_flat = temp[:].rearrange("p g t -> p (g t)")
             tau = once.tile([P, GROUPS * PACK], F32)
@@ -197,26 +211,21 @@ def tile_multiscalegeometricattention_kernel(
             )
             two_over_tau_sq = once.tile([P, GROUPS * PACK], F32)
             nc.vector.reciprocal(out=two_over_tau_sq[:], in_=half_tau_sq[:])
-
-            nc.vector.tensor_scalar_mul(out=half_x_sq[:], in0=x_sq[:], scalar1=0.5)
-            for half in range(ROW_HALVES):
-                spread = word_banks.tile([P, BANK], F32, tag="words")
-                for i in range(BANK // P):
-                    rt = half * (BANK // P) + i
-                    nc.tensor.transpose(
-                        spread[:, i * P : (i + 1) * P],
-                        half_x_sq[:, rt : rt + 1].to_broadcast([P, P]),
-                        ident[:],
-                    )
-                nc.vector.tensor_copy(
-                    out=half_x_sq_all[:, half * BANK : (half + 1) * BANK], in_=spread[:]
-                )
             finish_positions(0)
+
+            for t in range(PACK):
+                square_positions(1, t)
+                if t % 2 == 1:
+                    pack_positions(1, t // 2, nc.scalar.copy)
+            pos_tiles.append(load_positions(4))
 
             y_tiles = []
 
             def dot_products(g, j):
-                t, half = j // ROW_HALVES, j % ROW_HALVES
+                if g == GROUPS - 1:
+                    t, half = j % PACK, j // PACK
+                else:
+                    t, half = j // ROW_HALVES, j % ROW_HALVES
                 if half == 0:
                     y = y_pool.tile([P, ROWS], F32, tag="y")
                     y_tiles.append(y)
@@ -242,10 +251,10 @@ def tile_multiscalegeometricattention_kernel(
                     op1=ALU.subtract,
                 )
 
-            def clamp_and_scale(anchor):
+            def clamp_and_scale(anchor, rows=slice(0, ROWS)):
                 nc.vector.tensor_scalar(
-                    out=y_tiles[anchor][:],
-                    in0=y_tiles[anchor][:],
+                    out=y_tiles[anchor][:, rows],
+                    in0=y_tiles[anchor][:, rows],
                     scalar1=0.0,
                     scalar2=two_over_tau_sq[:, anchor : anchor + 1],
                     op0=ALU.max,
@@ -267,19 +276,34 @@ def tile_multiscalegeometricattention_kernel(
                 )
 
             all_dots = GROUPS * DOTS
+            turned_banks = [0]
             for first_unit in range(0, all_dots + TURN_LAG, RUN):
                 for unit in range(first_unit, first_unit + RUN):
                     s, j = unit // DOTS, unit % DOTS
                     if unit < all_dots:
                         dot_products(s, j)
-                    if ROW_HALVES <= unit <= all_dots and unit % ROW_HALVES == 0:
+                    last = unit - 1 - (all_dots - DOTS)
+                    if 0 <= last < DOTS:
+                        half = last // PACK
+                        clamp_and_scale(
+                            (GROUPS - 1) * PACK + last % PACK, slice(half * BANK, (half + 1) * BANK)
+                        )
+                    elif ROW_HALVES <= unit <= all_dots and unit % ROW_HALVES == 0:
                         clamp_and_scale(unit // ROW_HALVES - 1)
                     if j == DOTS // 2 and s + 1 < GROUPS:
                         finish_positions(s + 1)
                 for unit in range(first_unit, first_unit + RUN):
                     s, j = unit // DOTS, unit % DOTS
-                    if unit >= TURN_LAG:
-                        turn_and_root((unit - TURN_LAG) // DOTS, (unit - TURN_LAG) % DOTS)
+                    for _ in range(2 if unit >= CATCH_UP_FROM else 1):
+                        bank = turned_banks[0]
+                        g_, rt_ = bank // DOTS, bank % DOTS
+                        if g_ == GROUPS - 1:
+                            ready = g_ * DOTS + PACK * (rt_ // PACK + 1) + RUN
+                        else:
+                            ready = g_ * DOTS + TURN_LAG
+                        if bank < all_dots and unit >= ready:
+                            turn_and_root(g_, rt_)
+                            turned_banks[0] = bank + 1
                     if s + 2 < GROUPS and j % 2 == 0:
                         square_positions(s + 2, j // 2)
                     if s + 2 < GROUPS and j % 4 == 1:
@@ -315,15 +339,13 @@ def tile_multiscalegeometricattention_kernel(
                 return slice(pair * 2 * K_PASS, (pair + 1) * 2 * K_PASS)
 
             def exponentials(rt, pair):
-                nc.scalar.activation(
-                    out=z[rt][:, two_groups(pair)], in_=z[rt][:, two_groups(pair)], func=ACT.Exp,
-                    scale=-1.0, accum_out=part_sum[:, rt, pair : pair + 1],
-                )
+                if pair == 0:
+                    nc.scalar.activation(
+                        out=z[rt][:], in_=z[rt][:], func=ACT.Exp, scale=-1.0, accum_out=row_sum[:, rt : rt + 1],
+                    )
 
             def add_part_sums(rt):
-                nc.vector.reduce_sum(
-                    out=row_sum[:, rt : rt + 1], in_=part_sum[:, rt, :], axis=mybir.AxisListType.X
-                )
+                return
 
             def add_epsilon(rt):
                 nc.vector.tensor_scalar_add(
@@ -401,24 +423,39 @@ def tile_multiscalegeometricattention_kernel(
                 for pair in range(PAIRS):
                     exponentials(rt, pair)
             all_banks = ROW_TILES * PAIRS
-            for b in range(all_banks + LAG):
+            for b in range(all_banks):
                 rt, pair = b // PAIRS, b % PAIRS
                 next_sum = pair == PAIRS - 1 and rt + 1 < ROW_TILES
+                if b >= LAG:
+                    weigh_values((b - LAG) // PAIRS, (b - LAG) % PAIRS)
                 if rt + EXP_AHEAD < ROW_TILES:
                     exponentials(rt + EXP_AHEAD, pair)
-                if next_sum:
+                late_sum = next_sum and rt == 0
+                if next_sum and not late_sum:
                     add_part_sums(rt + 1)
                 if b < all_banks:
                     normalise(rt, pair)
                     turn_back(rt, pair)
-                if next_sum:
+                if next_sum and not late_sum:
                     add_epsilon(rt + 1)
                 copied = b - AHEAD - 1
                 if 0 <= copied < all_banks and copied % 2 == 1:
                     quantise(copied // PAIRS, copied % PAIRS)
                 if AHEAD <= b < all_banks + AHEAD:
                     copy_out((b - AHEAD) // PAIRS, (b - AHEAD) % PAIRS)
+                if late_sum:
+                    add_part_sums(rt + 1)
+                    add_epsilon(rt + 1)
                 if next_sum:
                     invert(rt + 1)
-                if b >= LAG:
-                    weigh_values((b - LAG) // PAIRS, (b - LAG) % PAIRS)
+
+            last = ROW_TILES - 1
+            copy_out(last, PAIRS - 2)
+            copy_out(last, PAIRS - 1)
+            quantise(last, 1)
+            weigh_values(last - 1, PAIRS - 1)
+            weigh_values(last, 0)
+            weigh_values(last, 1)
+            quantise(last, PAIRS - 1)
+            weigh_values(last, PAIRS - 2)
+            weigh_values(last, PAIRS - 1)

from contextlib import ExitStack

import concourse.mybir as mybir
from concourse.masks import make_identity

F32 = mybir.dt.float32
BF16 = mybir.dt.bfloat16
I32 = mybir.dt.int32
U32 = mybir.dt.uint32
U8 = mybir.dt.uint8
FP8X4 = mybir.dt.float8_e4m3fn_x4
ALU = mybir.AluOpType
ACT = mybir.ActivationFunctionType

P = 128
PACK = 4
K_PASS = P * PACK
ROWS = 1024
FEATURES = 512
ANCHORS = 4096
ROW_TILES = ROWS // P
GROUPS = ANCHORS // K_PASS
BANK = 512
ROW_HALVES = ROWS // BANK
DOTS = PACK * ROW_HALVES
RUN = 2
TURN_LAG = DOTS + RUN
EXP_AHEAD = 3
PAIRS = GROUPS // 2
AHEAD = 2
CATCH_UP_FROM = 56
LAG = AHEAD + 3

FLOPS = 2 * 2 * ROWS * ANCHORS * FEATURES


def every_second_word(tile_a, tile_b):
    words = (tile_a.bitcast(F32), tile_b.bitcast(F32))
    return [words[a][:, u : FEATURES // 2 : 2] for a in range(2) for u in range(2)]


def turn_words(nc, banks, ident, blocks):
    bank = banks.tile([P, 2, 2, P], F32, tag="words")
    for i, block in enumerate(blocks):
        nc.tensor.transpose(bank[:, i // 2, i % 2, :], block, ident)
    return bank


def words_side_by_side(copy, bank, grouped):
    copy(out=grouped.bitcast(F32), in_=bank[:].rearrange("p a u c -> p a c u"))


def tile_multiscalegeometricattention_kernel(
    tc, x, positions, values_words, values_scales, temperature, out
):
    nc = tc.nc
    x_rows = x.flatten_outer_dims()
    out_rows = out.flatten_outer_dims()

    with ExitStack() as whole:
        whole.enter_context(tc.manual_schedule())
        keep = whole.enter_context(tc.tile_pool(name="keep", bufs=1))

        ident = keep.tile([P, P], F32)
        make_identity(nc, ident[:])

        z = [keep.tile([P, ANCHORS], F32, name="z%d" % rt) for rt in range(ROW_TILES)]
        part_sum = keep.tile([P, ROW_TILES, PAIRS], F32)
        row_sum = keep.tile([P, ROW_TILES], F32)
        inverse = keep.tile([P, ROW_TILES], F32)

        v_words = keep.tile([P, GROUPS, FEATURES], U32, align_bytes=64)
        v_scales = keep.tile([P, GROUPS, FEATURES], U8, align_bytes=64)
        nc.vector.memset(v_scales[:].bitcast(I32), 0)

        with ExitStack() as first:
            once = first.enter_context(tc.tile_pool(name="once", bufs=1))
            loads = first.enter_context(tc.tile_pool(name="loads", bufs=3))
            stage = first.enter_context(tc.tile_pool(name="stage", bufs=2))
            word_banks = first.enter_context(tc.psum_pool(name="word_banks", bufs=2))
            dot_banks = first.enter_context(tc.psum_pool(name="dot_banks", bufs=3))
            turn_banks = first.enter_context(tc.psum_pool(name="turn_banks", bufs=3))

            warm = once.tile([P, 1], F32)
            nc.vector.memset(warm[:], 1.0)
            nc.scalar.activation(out=warm[:], in_=warm[:], func=ACT.Sqrt)

            def load_positions(g):
                pos = loads.tile([P, PACK, FEATURES], BF16, tag="pos")
                nc.sync.dma_start(
                    out=pos[:],
                    in_=positions[g * K_PASS : (g + 1) * K_PASS, :].rearrange(
                        "(p t) d -> p t d", t=PACK
                    ),
                )
                return pos

            x_sq = once.tile([P, ROW_TILES], F32)
            half_x_sq = once.tile([P, ROW_TILES], F32)
            half_x_sq_all = once.tile([P, ROWS], F32)
            x_codes = once.tile([P, ROWS], U32, align_bytes=64)
            x_scales = once.tile([P, ROWS], U8, align_bytes=64)
            temp = once.tile([P, GROUPS, PACK], BF16)
            pos_sq = once.tile([P, GROUPS * PACK], F32)
            half_pos_sq = once.tile([P, GROUPS * PACK], F32)
            pos_tiles = []
            grouped_tiles = []
            operands = []

            def square_positions(g, t):
                squares = stage.tile([P, FEATURES], BF16, tag="squares")
                nc.scalar.activation(
                    out=squares[:], in_=pos_tiles[g][:, t, :], func=ACT.Square,
                    accum_out=pos_sq[:, g * PACK + t : g * PACK + t + 1],
                )

            def pack_positions(g, pair, copy):
                if pair == 0:
                    grouped = stage.tile([P, PACK, P, PACK], BF16, tag="pos_grouped", align_bytes=64)
                    grouped_tiles.append(grouped)
                pos = pos_tiles[g]
                bank = turn_words(
                    nc, word_banks, ident[:],
                    every_second_word(pos[:, 2 * pair, :], pos[:, 2 * pair + 1, :]),
                )
                words_side_by_side(copy, bank, grouped_tiles[g][:, 2 * pair : 2 * pair + 2, :, :])

            def finish_positions(g):
                codes = stage.tile([P, K_PASS], U32, tag="pos_codes", align_bytes=64)
                scales = stage.tile([P, K_PASS], U8, tag="pos_scales", align_bytes=64)
                nc.vector.quantize_mx(
                    out=codes[:].bitcast(FP8X4),
                    scales=scales[:],
                    in_=grouped_tiles[g][:].rearrange("p a c t -> p (a c t)"),
                )
                operands.append((codes, scales))
                cols = slice(g * PACK, (g + 1) * PACK)
                nc.vector.tensor_scalar_mul(out=half_pos_sq[:, cols], in0=pos_sq[:, cols], scalar1=0.5)

            with tc.tile_pool(name="x_pool", bufs=1) as x_pool:
                x_sb = x_pool.tile([P, ROW_TILES, FEATURES], BF16)
                for rt in range(0, ROW_TILES, 2):
                    nc.sync.dma_start(
                        out=x_sb[:, rt : rt + 2, :],
                        in_=x_rows[rt * P : (rt + 2) * P, :].rearrange("(a p) d -> p a d", p=P),
                    )
                pos_tiles.append(load_positions(0))
                nc.sync.dma_start(
                    out=temp[:], in_=temperature.rearrange("(g p t) -> p g t", p=P, t=PACK)
                )
                pos_tiles.append(load_positions(1))
                pos_tiles.append(load_positions(2))

                x_grouped = x_pool.tile([P, ROW_TILES, P, PACK], BF16, align_bytes=64)
                for rt in range(0, ROW_TILES, 2):
                    bank = turn_words(
                        nc, word_banks, ident[:],
                        every_second_word(x_sb[:, rt, :], x_sb[:, rt + 1, :]),
                    )
                    words_side_by_side(nc.vector.tensor_copy, bank, x_grouped[:, rt : rt + 2, :, :])
                    squares = x_pool.tile([P, 2, FEATURES], BF16, tag="x_squares", bufs=2)
                    for a in range(2):
                        nc.scalar.activation(
                            out=squares[:, a, :], in_=x_sb[:, rt + a, :], func=ACT.Square,
                            accum_out=x_sq[:, rt + a : rt + a + 1],
                        )
                tiles_in_half = ROW_TILES // ROW_HALVES
                for half in range(ROW_HALVES):
                    nc.vector.quantize_mx(
                        out=x_codes[:, half * BANK : (half + 1) * BANK].bitcast(FP8X4),
                        scales=x_scales[:, half * BANK : (half + 1) * BANK],
                        in_=x_grouped[:, half * tiles_in_half : (half + 1) * tiles_in_half, :, :]
                        .rearrange("p a c t -> p (a c t)"),
                    )

            y_pool = first.enter_context(
                tc.tile_pool(name="y_pool", bufs=(TURN_LAG + DOTS) // ROW_HALVES + 1)
            )

            nc.vector.tensor_scalar_mul(out=half_x_sq[:], in0=x_sq[:], scalar1=0.5)
            for t in range(PACK):
                square_positions(0, t)
            for pair in range(PACK // 2):
                pack_positions(0, pair, nc.vector.tensor_copy)
            pos_tiles.append(load_positions(3))

            for half in range(ROW_HALVES):
                spread = word_banks.tile([P, BANK], F32, tag="words")
                for i in range(BANK // P):
                    rt = half * (BANK // P) + i
                    nc.tensor.transpose(
                        spread[:, i * P : (i + 1) * P],
                        half_x_sq[:, rt : rt + 1].to_broadcast([P, P]),
                        ident[:],
                    )
                nc.vector.tensor_copy(
                    out=half_x_sq_all[:, half * BANK : (half + 1) * BANK], in_=spread[:]
                )

            temp_flat = temp[:].rearrange("p g t -> p (g t)")
            tau = once.tile([P, GROUPS * PACK], F32)
            nc.vector.scalar_tensor_tensor(
                out=tau[:], in0=temp_flat, scalar=-1.0, in1=temp_flat, op0=ALU.mult, op1=ALU.max
            )
            nc.vector.tensor_scalar(
                out=tau[:], in0=tau[:], scalar1=0.1, scalar2=0.05, op0=ALU.add, op1=ALU.mult
            )
            half_tau_sq = once.tile([P, GROUPS * PACK], F32)
            nc.vector.scalar_tensor_tensor(
                out=half_tau_sq[:], in0=tau[:], scalar=0.5, in1=tau[:], op0=ALU.mult, op1=ALU.mult
            )
            two_over_tau_sq = once.tile([P, GROUPS * PACK], F32)
            nc.vector.reciprocal(out=two_over_tau_sq[:], in_=half_tau_sq[:])
            finish_positions(0)

            for t in range(PACK):
                square_positions(1, t)
                if t % 2 == 1:
                    pack_positions(1, t // 2, nc.scalar.copy)
            pos_tiles.append(load_positions(4))

            y_tiles = []

            def dot_products(g, j):
                if g == GROUPS - 1:
                    t, half = j % PACK, j // PACK
                else:
                    t, half = j // ROW_HALVES, j % ROW_HALVES
                if half == 0:
                    y = y_pool.tile([P, ROWS], F32, tag="y")
                    y_tiles.append(y)
                codes, scales = operands[g]
                anchor = g * PACK + t
                rows = slice(half * BANK, (half + 1) * BANK)
                dot = dot_banks.tile([P, BANK], F32, tag="dot")
                nc.tensor.matmul_mx(
                    out=dot[:],
                    lhsT=codes[:, t * P : (t + 1) * P].bitcast(FP8X4),
                    lhsT_scale=scales[:, t * P : (t + 1) * P],
                    rhs=x_codes[:, rows].bitcast(FP8X4),
                    rhs_scale=x_scales[:, rows],
                    start=True,
                    stop=True,
                )
                nc.vector.scalar_tensor_tensor(
                    out=y_tiles[anchor][:, rows],
                    in0=half_x_sq_all[:, rows],
                    scalar=half_pos_sq[:, anchor : anchor + 1],
                    in1=dot[:],
                    op0=ALU.add,
                    op1=ALU.subtract,
                )

            def clamp_and_scale(anchor, rows=slice(0, ROWS)):
                nc.vector.tensor_scalar(
                    out=y_tiles[anchor][:, rows],
                    in0=y_tiles[anchor][:, rows],
                    scalar1=0.0,
                    scalar2=two_over_tau_sq[:, anchor : anchor + 1],
                    op0=ALU.max,
                    op1=ALU.mult,
                )

            def turn_and_root(g, rt):
                turned = turn_banks.tile([P, PACK, P], F32, tag="turned")
                for t in range(PACK):
                    nc.tensor.transpose(
                        turned[:, t, :], y_tiles[g * PACK + t][:, rt * P : (rt + 1) * P], ident[:]
                    )
                nc.scalar.activation(
                    out=z[rt][:, g * K_PASS : (g + 1) * K_PASS].rearrange(
                        "r (u p e) -> r u p e", u=2, e=2
                    ),
                    in_=turned[:].rearrange("r (u e) p -> r u p e", e=2),
                    func=ACT.Sqrt,
                )

            all_dots = GROUPS * DOTS
            turned_banks = [0]
            for first_unit in range(0, all_dots + TURN_LAG, RUN):
                for unit in range(first_unit, first_unit + RUN):
                    s, j = unit // DOTS, unit % DOTS
                    if unit < all_dots:
                        dot_products(s, j)
                    last = unit - 1 - (all_dots - DOTS)
                    if 0 <= last < DOTS:
                        half = last // PACK
                        clamp_and_scale(
                            (GROUPS - 1) * PACK + last % PACK, slice(half * BANK, (half + 1) * BANK)
                        )
                    elif ROW_HALVES <= unit <= all_dots and unit % ROW_HALVES == 0:
                        clamp_and_scale(unit // ROW_HALVES - 1)
                    if j == DOTS // 2 and s + 1 < GROUPS:
                        finish_positions(s + 1)
                for unit in range(first_unit, first_unit + RUN):
                    s, j = unit // DOTS, unit % DOTS
                    for _ in range(2 if unit >= CATCH_UP_FROM else 1):
                        bank = turned_banks[0]
                        g_, rt_ = bank // DOTS, bank % DOTS
                        if g_ == GROUPS - 1:
                            ready = g_ * DOTS + PACK * (rt_ // PACK + 1) + RUN
                        else:
                            ready = g_ * DOTS + TURN_LAG
                        if bank < all_dots and unit >= ready:
                            turn_and_root(g_, rt_)
                            turned_banks[0] = bank + 1
                    if s + 2 < GROUPS and j % 2 == 0:
                        square_positions(s + 2, j // 2)
                    if s + 2 < GROUPS and j % 4 == 1:
                        pack_positions(s + 2, j // 4, nc.scalar.copy)
                    if s + 5 < GROUPS and j == DOTS - 1:
                        pos_tiles.append(load_positions(s + 5))

            nc.sync.dma_start(
                out=v_words[:].bitcast(I32),
                in_=values_words.rearrange("g p n t -> p g (n t)").bitcast(I32),
            )
            for quadrant in range(4):
                nc.sync.dma_start(
                    out=v_scales[32 * quadrant : 32 * quadrant + 4, :, :].bitcast(I32),
                    in_=values_scales[:, 4 * quadrant : 4 * quadrant + 4, :]
                    .rearrange("g q n -> q g n")
                    .bitcast(I32),
                )

        with ExitStack() as second:
            w_pool = second.enter_context(tc.tile_pool(name="w_pool", bufs=2))
            out_pool = second.enter_context(tc.tile_pool(name="out_pool", bufs=3))
            back_banks = second.enter_context(tc.psum_pool(name="back_banks", bufs=6))
            out_banks = second.enter_context(tc.psum_pool(name="out_banks", bufs=2))

            w_tiles = []
            w_grouped_tiles = []
            w_operands = []
            banks = []
            acc_tiles = []

            def two_groups(pair):
                return slice(pair * 2 * K_PASS, (pair + 1) * 2 * K_PASS)

            def exponentials(rt, pair):
                if pair == 0:
                    nc.scalar.activation(
                        out=z[rt][:], in_=z[rt][:], func=ACT.Exp, scale=-1.0, accum_out=row_sum[:, rt : rt + 1],
                    )

            def add_part_sums(rt):
                return

            def add_epsilon(rt):
                nc.vector.tensor_scalar_add(
                    out=row_sum[:, rt : rt + 1], in0=row_sum[:, rt : rt + 1], scalar1=1e-8
                )

            def invert(rt):
                nc.vector.reciprocal(out=inverse[:, rt : rt + 1], in_=row_sum[:, rt : rt + 1])

            def normalise(rt, pair):
                if pair == 0:
                    w = w_pool.tile([P, ANCHORS], BF16, tag="w")
                    w_tiles.append(w)
                nc.vector.tensor_scalar_mul(
                    out=w_tiles[rt][:, two_groups(pair)], in0=z[rt][:, two_groups(pair)],
                    scalar1=inverse[:, rt : rt + 1],
                )

            def turn_back(rt, pair):
                words = w_tiles[rt][:].bitcast(F32)
                blocks = [words[:, (4 * pair + i) * P : (4 * pair + i + 1) * P] for i in range(4)]
                banks.append(turn_words(nc, back_banks, ident[:], blocks))

            def copy_out(rt, pair):
                if pair == 0:
                    w_grouped = w_pool.tile([P, GROUPS, P, PACK], BF16, tag="w_grouped", align_bytes=64)
                    w_grouped_tiles.append(w_grouped)
                    w_codes = w_pool.tile([P, GROUPS * P], U32, tag="w_codes", align_bytes=64)
                    w_scales = w_pool.tile([P, GROUPS * P], U8, tag="w_scales", align_bytes=64)
                    w_operands.append((w_codes, w_scales))
                scalar_is_free = rt + EXP_AHEAD >= ROW_TILES
                copy = nc.scalar.copy if scalar_is_free else nc.vector.tensor_copy
                words_side_by_side(
                    copy, banks[rt * PAIRS + pair],
                    w_grouped_tiles[rt][:, 2 * pair : 2 * pair + 2, :, :],
                )

            def quantise(rt, pair):
                w_codes, w_scales = w_operands[rt]
                cols = slice((pair - 1) * 2 * P, (pair + 1) * 2 * P)
                nc.vector.quantize_mx(
                    out=w_codes[:, cols].bitcast(FP8X4),
                    scales=w_scales[:, cols],
                    in_=w_grouped_tiles[rt][:, 2 * pair - 2 : 2 * pair + 2, :, :].rearrange(
                        "p g r t -> p (g r t)"
                    ),
                )

            def weigh_values(rt, pair):
                if pair == 0:
                    acc = out_banks.tile([P, FEATURES], F32, tag="acc")
                    acc_tiles.append(acc)
                w_codes, w_scales = w_operands[rt]
                for g in range(2 * pair, 2 * pair + 2):
                    nc.tensor.matmul_mx(
                        out=acc_tiles[rt][:],
                        lhsT=w_codes[:, g * P : (g + 1) * P].bitcast(FP8X4),
                        lhsT_scale=w_scales[:, g * P : (g + 1) * P],
                        rhs=v_words[:, g, :].bitcast(FP8X4),
                        rhs_scale=v_scales[:, g, :],
                        start=(g == 0),
                        stop=(g == GROUPS - 1),
                    )
                if pair == PAIRS - 1:
                    result = out_pool.tile([P, FEATURES], F32, tag="result")
                    nc.scalar.copy(out=result[:], in_=acc_tiles[rt][:])
                    nc.sync.dma_start(out=out_rows[rt * P : (rt + 1) * P, :], in_=result[:])

            for pair in range(PAIRS):
                exponentials(0, pair)
            add_part_sums(0)
            add_epsilon(0)
            invert(0)
            for rt in range(1, EXP_AHEAD):
                for pair in range(PAIRS):
                    exponentials(rt, pair)
            all_banks = ROW_TILES * PAIRS
            for b in range(all_banks):
                rt, pair = b // PAIRS, b % PAIRS
                next_sum = pair == PAIRS - 1 and rt + 1 < ROW_TILES
                if b >= LAG:
                    weigh_values((b - LAG) // PAIRS, (b - LAG) % PAIRS)
                if rt + EXP_AHEAD < ROW_TILES:
                    exponentials(rt + EXP_AHEAD, pair)
                late_sum = next_sum and rt == 0
                if next_sum and not late_sum:
                    add_part_sums(rt + 1)
                if b < all_banks:
                    normalise(rt, pair)
                    turn_back(rt, pair)
                if next_sum and not late_sum:
                    add_epsilon(rt + 1)
                copied = b - AHEAD - 1
                if 0 <= copied < all_banks and copied % 2 == 1:
                    quantise(copied // PAIRS, copied % PAIRS)
                if AHEAD <= b < all_banks + AHEAD:
                    copy_out((b - AHEAD) // PAIRS, (b - AHEAD) % PAIRS)
                if late_sum:
                    add_part_sums(rt + 1)
                    add_epsilon(rt + 1)
                if next_sum:
                    invert(rt + 1)

            last = ROW_TILES - 1
            copy_out(last, PAIRS - 2)
            copy_out(last, PAIRS - 1)
            quantise(last, 1)
            weigh_values(last - 1, PAIRS - 1)
            weigh_values(last, 0)
            weigh_values(last, 1)
            quantise(last, PAIRS - 1)
            weigh_values(last, PAIRS - 2)
            weigh_values(last, PAIRS - 1)
